import numpy as np
import ml_dtypes


def mxq(x, axis, fmt="e4m3"):
    dtype, down = {"e4m3": (ml_dtypes.float8_e4m3fn, 7), "e5m2": (ml_dtypes.float8_e5m2, 14)}[fmt]
    v = np.moveaxis(np.asarray(x, np.float32).astype(ml_dtypes.bfloat16).astype(np.float64), axis, -1)
    blocks = v.reshape(v.shape[:-1] + (-1, 32))
    amax = np.abs(blocks).max(-1, keepdims=True)
    byte = np.maximum(np.where(amax > 0, np.frexp(amax)[1] - 1 + 127, 0) - down, 1)
    scale = np.exp2(byte - 127.0)
    codes = (blocks / scale).astype(np.float32).astype(dtype).astype(np.float64)
    return np.moveaxis((codes * scale).reshape(v.shape), -1, axis)


WIDE = False


def mx_kscale(k):
    if not WIDE:
        return np.ones(k)
    levels = np.array([10, -10, 5, -5, 0])
    if k % 512:
        return np.exp2(np.random.permutation(np.resize(levels, k // 32))).repeat(32)
    a = np.empty((k // 512, 16))
    for p in range(k // 512):
        a[p, :8] = np.random.permutation(np.resize(levels, 8))
        for g in range(8):
            far = levels[np.abs(levels - a[p, g]) >= 10]
            a[p, g + 8] = far[np.random.randint(len(far))]
    return np.exp2(a.ravel()).repeat(32)


BF16 = ml_dtypes.bfloat16


def bf(x):
    return np.asarray(x, np.float32).astype(BF16)


def f64(x):
    return np.asarray(x).astype(np.float64)


B, S, I0, I1, I2, I3, I4, O0, O1, O2, O3, O4, R1, R2, R3, R4 = 4, 2048, 4, 4, 2, 2, 16, 2, 2, 2, 2, 8, 16, 512, 1024, 512
IL, OL = I0 * I1 * I2 * I3, O0 * O1 * O2 * O3
IN, OUT = IL * I4, OL * O4


def setup_inputs():
    s = mx_kscale(R4)
    a = mx_kscale(IN)[::I4]
    return {"x": bf(np.random.standard_normal((B, S, IN)) / np.repeat(a, I4)),
            "t3": bf(np.random.standard_normal((IL, OL, R4)) * s * a[:, None, None]),
            "core4": bf(np.random.standard_normal((R4, I4, O4, 1)) / np.sqrt(R4 * IN) / s[:, None, None, None]),
            "bias": bf(np.random.standard_normal(OUT))}


def reference(x, t3, core4, bias):
    p = mxq(f64(t3).reshape(IL * OL, R4), 1, "e4m3") @ mxq(f64(core4).reshape(R4, I4 * O4), 0, "e4m3")
    m = p.reshape(IL, OL, I4, O4, 1).transpose(0, 2, 1, 3, 4).reshape(IN, OUT, 1)[:, :, 0]
    y = (mxq(f64(x).reshape(B * S, IN), 1, "e4m3") @ mxq(m, 0, "e4m3")) + f64(bias)
    return y.reshape(B, S, OUT)

@@ -1,0 +1,262 @@
+from contextlib import ExitStack
+
+import concourse.mybir as mybir
+from concourse.masks import make_identity
+
+F32 = mybir.dt.float32
+BF16 = mybir.dt.bfloat16
+U32 = mybir.dt.uint32
+U8 = mybir.dt.uint8
+I32 = mybir.dt.int32
+FP8X4 = mybir.dt.float8_e4m3fn_x4
+ADD = mybir.AluOpType.add
+
+P = 128
+FLOPS = 2 * 1024 * 512 * 128 + 2 * 8192 * 1024 * 128
+UNITS = tuple((4 * c, 4) for c in range(15)) + ((60, 2), (62, 2))
+N_UNITS = len(UNITS)
+LAST_FULL = 14
+X_BUFS = 10
+STORE_AFTER = {3: 0, 7: 4, 11: 8, 13: 12, 14: 14, 16: 15}
+
+
+def tile_linear2mpo_pb_t_kernel(tc, x, t3, core4, bias, out):
+    nc = tc.nc
+    with ExitStack() as ctx:
+        const = ctx.enter_context(tc.tile_pool(name="const", bufs=1))
+        xpool = ctx.enter_context(tc.tile_pool(name="xpool", bufs=X_BUFS))
+        ppool = ctx.enter_context(tc.tile_pool(name="ppool", bufs=2))
+        gpool = ctx.enter_context(tc.tile_pool(name="gpool", bufs=3))
+        cpool = ctx.enter_context(tc.tile_pool(name="cpool", bufs=6))
+        ps_t = ctx.enter_context(tc.psum_pool(name="ps_t", bufs=6))
+        ps_y = ctx.enter_context(tc.psum_pool(name="ps_y", bufs=2))
+        ctx.enter_context(tc.manual_schedule())
+
+        x_v = x.rearrange("b (q t) k -> (b q) (t k)", t=64)
+        out_v = out.rearrange("b (q t) n -> (b q) (t n)", t=64)
+        t3_v = t3.rearrange("a (h s) r -> (a h) (s r)", h=2)
+        c4_v = core4.rearrange("(q t) i o z -> q (t i o z)", t=4)
+        bias_v = bias.rearrange("(o n) -> o n", o=1)
+
+        idf = const.tile([P, P], F32, name="idf")
+        make_identity(nc, idf[:])
+        idb = const.tile([P, P], BF16, name="idb")
+        make_identity(nc, idb[:])
+        bias_row = const.tile([P, 512], BF16, name="bias_row")
+        nc.vector.memset(bias_row[:], 0.0)
+        ones = const.tile([P, P], BF16, name="ones")
+        nc.vector.memset(ones[:], 1.0)
+        t3_codes = const.tile([P, 1088], U32, name="t3_codes", align_bytes=64)
+        t3_scales = const.tile([P, 1088], U8, name="t3_scales", align_bytes=64)
+        nc.vector.memset(t3_codes[:, 1024:1088].bitcast(I32), 0)
+        nc.vector.memset(t3_scales[:, 1024:1088].bitcast(I32), 0)
+
+        c4raw = const.tile([P, 512], BF16, name="c4raw")
+        t3_sb = const.tile([P, 4096], BF16, name="t3_sb")
+        for sp in range(4):
+            nc.sync.dma_start(out=t3_sb[:, 1024 * sp : 1024 * (sp + 1)], in_=t3_v[:, 1024 * sp : 1024 * (sp + 1)])
+            if sp == 0:
+                nc.sync.dma_start(out=c4raw[:], in_=c4_v)
+        nc.scalar.dma_start(out=bias_row[0:1, 0:128], in_=bias_v)
+
+        x_tiles = {}
+
+        def load_x(u):
+            if u < N_UNITS:
+                t0, nt = UNITS[u]
+                x_sb = xpool.tile([P, 4096], BF16, name="x_sb", tag="x_sb")
+                nc.sync.dma_start(out=x_sb[:, 0 : 1024 * nt], in_=x_v[:, 1024 * t0 : 1024 * (t0 + nt)])
+                x_tiles[u] = x_sb
+
+        for u in range(X_BUFS):
+            load_x(u)
+
+        gc4 = const.tile([P, 512], BF16, name="gc4", align_bytes=64)
+        for e in range(2):
+            nc.vector.tensor_copy(
+                out=gc4[:].rearrange("p (o e h t) -> p e o h t", o=8, e=2, h=8, t=4)[:, e],
+                in_=c4raw[:].rearrange("p (t h e o) -> p e o h t", t=4, h=8, e=2, o=8)[:, e],
+            )
+        c4_codes = const.tile([P, 128], U32, name="c4_codes", align_bytes=64)
+        c4_scales = const.tile([P, 128], U8, name="c4_scales", align_bytes=64)
+        nc.vector.quantize_mx(out=c4_codes[:].bitcast(FP8X4), scales=c4_scales[:], in_=gc4[:])
+
+        t3w = t3_sb[:].bitcast(F32)
+        gt3 = const.tile([P, 4096], BF16, name="gt3", align_bytes=64)
+        gt3w = gt3[:].bitcast(F32)
+        for sp in range(4):
+            tp = ps_t.tile([P, 512], F32, name="tp", tag="xt")
+            for w in range(4):
+                s, u = 2 * sp + w // 2, w % 2
+                nc.tensor.transpose(
+                    out=tp[:, 128 * w : 128 * (w + 1)],
+                    in_=t3w[:, 256 * s + u : 256 * (s + 1) : 2],
+                    identity=idf[:],
+                )
+            dst = gt3w.rearrange("p (b x sp w) -> p sp b x w", b=16, x=8, sp=4, w=4)[:, sp]
+            src = tp[:].rearrange("p (w b x) -> p b x w", w=4, b=16, x=8)
+            if sp % 2 == 0:
+                nc.vector.tensor_copy(out=dst, in_=src)
+            else:
+                nc.scalar.copy(out=dst, in_=src)
+        for jh in range(2):
+            nc.vector.quantize_mx(
+                out=t3_codes[:, 512 * jh : 512 * (jh + 1)].bitcast(FP8X4),
+                scales=t3_scales[:, 512 * jh : 512 * (jh + 1)],
+                in_=gt3[:, 2048 * jh : 2048 * (jh + 1)],
+            )
+
+        yb = ps_y.tile([P, 512], F32, name="yb", tag="y")
+        nc.tensor.matmul(out=yb[:], lhsT=ones[:], rhs=bias_row[:], start=True, stop=True)
+        bias_bc = const.tile([P, 512], F32, name="bias_bc")
+        for k in range(4):
+            nc.scalar.copy(out=bias_bc[:, 128 * k : 128 * (k + 1)], in_=yb[:, 0:128])
+
+        pm = const.tile([P, 2048], BF16, name="pm")
+        for b in range(4):
+            if b < 2:
+                sp = ps_y.tile([P, 512], F32, name="sp", tag="y")
+            else:
+                sp = ps_t.tile([P, 512], F32, name="sp2", tag="xt")
+            for jq in range(4):
+                j = 4 * b + jq
+                nc.tensor.matmul_mx(
+                    out=sp[:, 128 * jq : 128 * (jq + 1)],
+                    lhsT=t3_codes[:, 64 * j : 64 * j + 128].bitcast(FP8X4),
+                    lhsT_scale=t3_scales[:, 64 * j : 64 * j + 128],
+                    rhs=c4_codes[:].bitcast(FP8X4),
+                    rhs_scale=c4_scales[:],
+                    start=True,
+                    stop=True,
+                )
+            nc.vector.tensor_copy(
+                out=pm[:].rearrange("p (tr b jq h) -> p b tr jq h", tr=16, b=4, jq=4, h=8)[:, b],
+                in_=sp[:].rearrange("p (jq tr h) -> p tr jq h", jq=4, tr=16, h=8),
+            )
+
+        grouped = {}
+        codes = {}
+        y_tiles = {}
+        out_sb = const.tile([P, 8192], F32, name="out_sb")
+
+        permuted = {}
+
+        def permute_unit(u):
+            if u >= N_UNITS:
+                return
+            nt = UNITS[u][1]
+            x_perm = ppool.tile([P, 4096], BF16, name="x_perm", tag="x_perm", align_bytes=64)
+            nc.vector.tensor_copy(
+                out=x_perm[:, 0 : 1024 * nt].rearrange("p (t v b j) -> p t v b j", v=4, b=16, j=16),
+                in_=x_tiles[u][:, 0 : 1024 * nt].rearrange("p (t b v j) -> p t v b j", b=16, v=4, j=16),
+            )
+            permuted[u] = x_perm
+            load_x(u + X_BUFS)
+
+        def transpose_unit(u):
+            nt = UNITS[u][1]
+            xw = permuted[u][:].bitcast(F32)
+            g_sb = gpool.tile([P, 4096], BF16, name="g_sb", tag="g_sb", align_bytes=64)
+            gw = g_sb[:].bitcast(F32)
+            for t in range(nt):
+                bank = ps_t.tile([P, 512], F32, name="xt", tag="xt")
+                for a in range(4):
+                    w0 = 512 * t + 128 * a
+                    nc.tensor.transpose(
+                        out=bank[:, 128 * a : 128 * (a + 1)], in_=xw[:, w0 : w0 + 128], identity=idf[:]
+                    )
+                dst = gw[:, 512 * t : 512 * (t + 1)].rearrange("p (g r u) -> p g r u", g=2, r=128, u=2)
+                src = bank[:].rearrange("p (g u r) -> p g r u", g=2, u=2, r=128)
+                nc.scalar.copy(out=dst, in_=src)
+            grouped[u] = g_sb
+
+        def quantise_unit(u):
+            nt = UNITS[u][1]
+            x_codes = cpool.tile([P, 1024], U32, name="x_codes", tag="x_codes", align_bytes=64)
+            x_scales = cpool.tile([P, 1024], U8, name="x_scales", tag="x_scales", align_bytes=64)
+            nc.vector.quantize_mx(
+                out=x_codes[:, 0 : 256 * nt].bitcast(FP8X4),
+                scales=x_scales[:, 0 : 256 * nt],
+                in_=grouped[u][:, 0 : 1024 * nt],
+            )
+            codes[u] = (x_codes, x_scales)
+
+        def multiply_unit(u):
+            nt = UNITS[u][1]
+            x_codes, x_scales = codes[u]
+            y = ps_y.tile([P, 512], F32, name="y", tag="y")
+            for t in range(nt):
+                for g in range(2):
+                    s0 = 128 * (2 * t + g)
+                    nc.tensor.matmul_mx(
+                        out=y[:, 128 * t : 128 * (t + 1)],
+                        lhsT=x_codes[:, s0 : s0 + 128].bitcast(FP8X4),
+                        lhsT_scale=x_scales[:, s0 : s0 + 128],
+                        rhs=m_codes[:, 128 * g : 128 * (g + 1)].bitcast(FP8X4),
+                        rhs_scale=m_scales[:, 128 * g : 128 * (g + 1)],
+                        start=(g == 0),
+                        stop=(g == 1),
+                    )
+            y_tiles[u] = y
+
+        def finish_unit(u):
+            t0, nt = UNITS[u]
+            nc.vector.tensor_tensor(
+                out=out_sb[:, 128 * t0 : 128 * (t0 + nt)],
+                in0=y_tiles[u][:, 0 : 128 * nt],
+                in1=bias_bc[:, 0 : 128 * nt],
+                op=ADD,
+            )
+            if u in STORE_AFTER:
+                lo = 128 * UNITS[STORE_AFTER[u]][0]
+                hi = 128 * (t0 + nt)
+                nc.sync.dma_start(out=out_v[:, lo:hi], in_=out_sb[:, lo:hi])
+
+        permute_unit(0)
+        transpose_unit(0)
+
+        gm = const.tile([P, 1024], BF16, name="gm", align_bytes=64)
+        for ob in range(2):
+            mp = ps_t.tile([P, 1024], BF16, name="mp", tag="xt")
+            for trl in range(8):
+                tr = 8 * ob + trl
+                nc.tensor.transpose(
+                    out=mp[:, 128 * trl : 128 * (trl + 1)], in_=pm[:, 128 * tr : 128 * (tr + 1)], identity=idb[:]
+                )
+            for e in range(2):
+                nc.vector.tensor_copy(
+                    out=gm[:].rearrange("p (g q ob ol u e) -> p ob e g q ol u", g=2, q=16, ob=2, ol=4, u=2, e=2)[:, ob, e],
+                    in_=mp[:].rearrange("p (ol e d g u q) -> p e d g q ol u", ol=4, e=2, d=2, g=2, u=2, q=16)[:, e, 0],
+                )
+        m_codes = const.tile([P, 256], U32, name="m_codes", align_bytes=64)
+        m_scales = const.tile([P, 256], U8, name="m_scales", align_bytes=64)
+        nc.vector.quantize_mx(out=m_codes[:].bitcast(FP8X4), scales=m_scales[:], in_=gm[:])
+
+        permute_unit(1)
+        transpose_unit(1)
+        quantise_unit(0)
+        permute_unit(2)
+
+        for i in range(2, LAST_FULL + 1):
+            transpose_unit(i)
+            if i >= 3:
+                finish_unit(i - 3)
+            quantise_unit(i - 1)
+            permute_unit(i + 1)
+            multiply_unit(i - 2)
+
+        permute_unit(16)
+        transpose_unit(15)
+        transpose_unit(16)
+        finish_unit(12)
+        quantise_unit(14)
+        multiply_unit(13)
+        multiply_unit(14)
+        quantise_unit(15)
+        finish_unit(13)
+        quantise_unit(16)
+        multiply_unit(15)
+        multiply_unit(16)
+        finish_unit(14)
+        finish_unit(15)
+        finish_unit(16)

@@ -15,9 +15,9 @@ P = 128
 FLOPS = 2 * 1024 * 512 * 128 + 2 * 8192 * 1024 * 128
 UNITS = tuple((4 * c, 4) for c in range(15)) + ((60, 2), (62, 2))
 N_UNITS = len(UNITS)
-LAST_FULL = 14
 X_BUFS = 10
-STORE_AFTER = {3: 0, 7: 4, 11: 8, 13: 12, 14: 14, 16: 15}
+SCALAR_PERMUTES = (1, 2, 4, 5, 7, 8, 10, 11, 13, 14)
+STORE_AFTER = {5: 0, 8: 6, 10: 9, 12: 11, 13: 13, 14: 14, 15: 15, 16: 16}
 
 
 def tile_linear2mpo_pb_t_kernel(tc, x, t3, core4, bias, out):
@@ -42,133 +42,96 @@ def tile_linear2mpo_pb_t_kernel(tc, x, t3, core4, bias, out):
         make_identity(nc, idf[:])
         idb = const.tile([P, P], BF16, name="idb")
         make_identity(nc, idb[:])
-        bias_row = const.tile([P, 512], BF16, name="bias_row")
+        bias_row = const.tile([P, P], BF16, name="bias_row")
         nc.vector.memset(bias_row[:], 0.0)
         ones = const.tile([P, P], BF16, name="ones")
         nc.vector.memset(ones[:], 1.0)
+        warm = const.tile([P, 16], BF16, name="warm")
+        nc.scalar.copy(out=warm[:], in_=ones[:, 0:16])
         t3_codes = const.tile([P, 1088], U32, name="t3_codes", align_bytes=64)
         t3_scales = const.tile([P, 1088], U8, name="t3_scales", align_bytes=64)
         nc.vector.memset(t3_codes[:, 1024:1088].bitcast(I32), 0)
         nc.vector.memset(t3_scales[:, 1024:1088].bitcast(I32), 0)
 
-        c4raw = const.tile([P, 512], BF16, name="c4raw")
-        t3_sb = const.tile([P, 4096], BF16, name="t3_sb")
-        for sp in range(4):
-            nc.sync.dma_start(out=t3_sb[:, 1024 * sp : 1024 * (sp + 1)], in_=t3_v[:, 1024 * sp : 1024 * (sp + 1)])
-            if sp == 0:
-                nc.sync.dma_start(out=c4raw[:], in_=c4_v)
-        nc.scalar.dma_start(out=bias_row[0:1, 0:128], in_=bias_v)
-
         x_tiles = {}
+
+        def new_x(u):
+            x_tiles[u] = xpool.tile([P, 4096], BF16, name="x_sb", tag="x_sb")
+
+        def load_x_tiles(u, lo, hi):
+            t0 = UNITS[u][0]
+            nc.sync.dma_start(
+                out=x_tiles[u][:, 1024 * lo : 1024 * hi], in_=x_v[:, 1024 * (t0 + lo) : 1024 * (t0 + hi)]
+            )
 
         def load_x(u):
             if u < N_UNITS:
-                t0, nt = UNITS[u]
-                x_sb = xpool.tile([P, 4096], BF16, name="x_sb", tag="x_sb")
-                nc.sync.dma_start(out=x_sb[:, 0 : 1024 * nt], in_=x_v[:, 1024 * t0 : 1024 * (t0 + nt)])
-                x_tiles[u] = x_sb
+                new_x(u)
+                load_x_tiles(u, 0, UNITS[u][1])
 
-        for u in range(X_BUFS):
+        new_x(0)
+        for t in range(4):
+            load_x_tiles(0, t, t + 1)
+        nc.sync.dma_start(out=bias_row[0:1, :], in_=bias_v)
+        c4raw = const.tile([P, 512], BF16, name="c4raw")
+        nc.sync.dma_start(out=c4raw[:], in_=c4_v)
+        t3_sb = const.tile([P, 4096], BF16, name="t3_sb")
+        for sp in range(4):
+            nc.sync.dma_start(out=t3_sb[:, 1024 * sp : 1024 * (sp + 1)], in_=t3_v[:, 1024 * sp : 1024 * (sp + 1)])
+        for u in range(1, X_BUFS):
             load_x(u)
 
-        gc4 = const.tile([P, 512], BF16, name="gc4", align_bytes=64)
-        for e in range(2):
-            nc.vector.tensor_copy(
-                out=gc4[:].rearrange("p (o e h t) -> p e o h t", o=8, e=2, h=8, t=4)[:, e],
-                in_=c4raw[:].rearrange("p (t h e o) -> p e o h t", t=4, h=8, e=2, o=8)[:, e],
-            )
-        c4_codes = const.tile([P, 128], U32, name="c4_codes", align_bytes=64)
-        c4_scales = const.tile([P, 128], U8, name="c4_scales", align_bytes=64)
-        nc.vector.quantize_mx(out=c4_codes[:].bitcast(FP8X4), scales=c4_scales[:], in_=gc4[:])
-
-        t3w = t3_sb[:].bitcast(F32)
-        gt3 = const.tile([P, 4096], BF16, name="gt3", align_bytes=64)
-        gt3w = gt3[:].bitcast(F32)
-        for sp in range(4):
-            tp = ps_t.tile([P, 512], F32, name="tp", tag="xt")
-            for w in range(4):
-                s, u = 2 * sp + w // 2, w % 2
-                nc.tensor.transpose(
-                    out=tp[:, 128 * w : 128 * (w + 1)],
-                    in_=t3w[:, 256 * s + u : 256 * (s + 1) : 2],
-                    identity=idf[:],
-                )
-            dst = gt3w.rearrange("p (b x sp w) -> p sp b x w", b=16, x=8, sp=4, w=4)[:, sp]
-            src = tp[:].rearrange("p (w b x) -> p b x w", w=4, b=16, x=8)
-            if sp % 2 == 0:
-                nc.vector.tensor_copy(out=dst, in_=src)
-            else:
-                nc.scalar.copy(out=dst, in_=src)
-        for jh in range(2):
-            nc.vector.quantize_mx(
-                out=t3_codes[:, 512 * jh : 512 * (jh + 1)].bitcast(FP8X4),
-                scales=t3_scales[:, 512 * jh : 512 * (jh + 1)],
-                in_=gt3[:, 2048 * jh : 2048 * (jh + 1)],
-            )
-
-        yb = ps_y.tile([P, 512], F32, name="yb", tag="y")
-        nc.tensor.matmul(out=yb[:], lhsT=ones[:], rhs=bias_row[:], start=True, stop=True)
-        bias_bc = const.tile([P, 512], F32, name="bias_bc")
-        for k in range(4):
-            nc.scalar.copy(out=bias_bc[:, 128 * k : 128 * (k + 1)], in_=yb[:, 0:128])
-
-        pm = const.tile([P, 2048], BF16, name="pm")
-        for b in range(4):
-            if b < 2:
-                sp = ps_y.tile([P, 512], F32, name="sp", tag="y")
-            else:
-                sp = ps_t.tile([P, 512], F32, name="sp2", tag="xt")
-            for jq in range(4):
-                j = 4 * b + jq
-                nc.tensor.matmul_mx(
-                    out=sp[:, 128 * jq : 128 * (jq + 1)],
-                    lhsT=t3_codes[:, 64 * j : 64 * j + 128].bitcast(FP8X4),
-                    lhsT_scale=t3_scales[:, 64 * j : 64 * j + 128],
-                    rhs=c4_codes[:].bitcast(FP8X4),
-                    rhs_scale=c4_scales[:],
-                    start=True,
-                    stop=True,
-                )
-            nc.vector.tensor_copy(
-                out=pm[:].rearrange("p (tr b jq h) -> p b tr jq h", tr=16, b=4, jq=4, h=8)[:, b],
-                in_=sp[:].rearrange("p (jq tr h) -> p tr jq h", jq=4, tr=16, h=8),
-            )
-
+        permuted = {}
         grouped = {}
         codes = {}
         y_tiles = {}
         out_sb = const.tile([P, 8192], F32, name="out_sb")
 
-        permuted = {}
+        def new_permuted(u):
+            permuted[u] = ppool.tile([P, 4096], BF16, name="x_perm", tag="x_perm", align_bytes=64)
+
+        def vector_permute(u, lo, hi):
+            nc.vector.tensor_copy(
+                out=permuted[u][:, 1024 * lo : 1024 * hi].rearrange("p (t v b j) -> p v t b j", v=4, b=16, j=16),
+                in_=x_tiles[u][:, 1024 * lo : 1024 * hi].rearrange("p (t b v j) -> p v t b j", b=16, v=4, j=16),
+            )
+
+        def scalar_permute(u, t):
+            nc.scalar.copy(
+                out=permuted[u][:, 1024 * t : 1024 * (t + 1)].bitcast(F32).rearrange("p (v b j) -> p v b j", v=4, b=16, j=8),
+                in_=x_tiles[u][:, 1024 * t : 1024 * (t + 1)].bitcast(F32).rearrange("p (b v j) -> p v b j", b=16, v=4, j=8),
+            )
 
         def permute_unit(u):
-            if u >= N_UNITS:
-                return
-            nt = UNITS[u][1]
-            x_perm = ppool.tile([P, 4096], BF16, name="x_perm", tag="x_perm", align_bytes=64)
-            nc.vector.tensor_copy(
-                out=x_perm[:, 0 : 1024 * nt].rearrange("p (t v b j) -> p t v b j", v=4, b=16, j=16),
-                in_=x_tiles[u][:, 0 : 1024 * nt].rearrange("p (t b v j) -> p t v b j", b=16, v=4, j=16),
+            if u < N_UNITS:
+                new_permuted(u)
+                nt = UNITS[u][1]
+                if u in SCALAR_PERMUTES:
+                    vector_permute(u, 0, nt - 1)
+                    scalar_permute(u, nt - 1)
+                else:
+                    vector_permute(u, 0, nt)
+                load_x(u + X_BUFS)
+
+        def transpose_tile(u, t, copy):
+            xw = permuted[u][:].bitcast(F32)
+            bank = ps_t.tile([P, 512], F32, name="xt", tag="xt")
+            for a in range(4):
+                w0 = 512 * t + 128 * a
+                nc.tensor.transpose(out=bank[:, 128 * a : 128 * (a + 1)], in_=xw[:, w0 : w0 + 128], identity=idf[:])
+            gw = grouped[u][:].bitcast(F32)
+            copy(
+                out=gw[:, 512 * t : 512 * (t + 1)].rearrange("p (g r u) -> p g r u", g=2, r=128, u=2),
+                in_=bank[:].rearrange("p (g u r) -> p g r u", g=2, u=2, r=128),
             )
-            permuted[u] = x_perm
-            load_x(u + X_BUFS)
+
+        def new_grouped(u):
+            grouped[u] = gpool.tile([P, 4096], BF16, name="g_sb", tag="g_sb", align_bytes=64)
 
         def transpose_unit(u):
-            nt = UNITS[u][1]
-            xw = permuted[u][:].bitcast(F32)
-            g_sb = gpool.tile([P, 4096], BF16, name="g_sb", tag="g_sb", align_bytes=64)
-            gw = g_sb[:].bitcast(F32)
-            for t in range(nt):
-                bank = ps_t.tile([P, 512], F32, name="xt", tag="xt")
-                for a in range(4):
-                    w0 = 512 * t + 128 * a
-                    nc.tensor.transpose(
-                        out=bank[:, 128 * a : 128 * (a + 1)], in_=xw[:, w0 : w0 + 128], identity=idf[:]
-                    )
-                dst = gw[:, 512 * t : 512 * (t + 1)].rearrange("p (g r u) -> p g r u", g=2, r=128, u=2)
-                src = bank[:].rearrange("p (g u r) -> p g r u", g=2, u=2, r=128)
-                nc.scalar.copy(out=dst, in_=src)
-            grouped[u] = g_sb
+            new_grouped(u)
+            for t in range(UNITS[u][1]):
+                transpose_tile(u, t, nc.scalar.copy)
 
         def quantise_unit(u):
             nt = UNITS[u][1]
@@ -202,9 +165,9 @@ def tile_linear2mpo_pb_t_kernel(tc, x, t3, core4, bias, out):
         def finish_unit(u):
             t0, nt = UNITS[u]
             nc.vector.tensor_tensor(
-                out=out_sb[:, 128 * t0 : 128 * (t0 + nt)],
-                in0=y_tiles[u][:, 0 : 128 * nt],
-                in1=bias_bc[:, 0 : 128 * nt],
+                out=out_sb[:, 128 * t0 : 128 * (t0 + nt)].rearrange("p (t n) -> p t n", n=128),
+                in0=y_tiles[u][:, 0 : 128 * nt].rearrange("p (t n) -> p t n", n=128),
+                in1=bias_bc[:].unsqueeze(1).to_broadcast([P, nt, 128]),
                 op=ADD,
             )
             if u in STORE_AFTER:
@@ -212,8 +175,77 @@ def tile_linear2mpo_pb_t_kernel(tc, x, t3, core4, bias, out):
                 hi = 128 * (t0 + nt)
                 nc.sync.dma_start(out=out_v[:, lo:hi], in_=out_sb[:, lo:hi])
 
-        permute_unit(0)
-        transpose_unit(0)
+        new_permuted(0)
+        new_grouped(0)
+        for t in range(4):
+            vector_permute(0, t, t + 1)
+            transpose_tile(0, t, nc.scalar.copy)
+        load_x(X_BUFS)
+
+        gc4 = const.tile([P, 512], BF16, name="gc4", align_bytes=64)
+        for e in range(2):
+            nc.vector.tensor_copy(
+                out=gc4[:].rearrange("p (o e h t) -> p e o h t", o=8, e=2, h=8, t=4)[:, e],
+                in_=c4raw[:].rearrange("p (t h e o) -> p e o h t", t=4, h=8, e=2, o=8)[:, e],
+            )
+        c4_codes = const.tile([P, 128], U32, name="c4_codes", align_bytes=64)
+        c4_scales = const.tile([P, 128], U8, name="c4_scales", align_bytes=64)
+        nc.vector.quantize_mx(out=c4_codes[:].bitcast(FP8X4), scales=c4_scales[:], in_=gc4[:])
+
+        t3w = t3_sb[:].bitcast(F32)
+        gt3 = const.tile([P, 4096], BF16, name="gt3", align_bytes=64)
+        gt3w = gt3[:].bitcast(F32)
+        for sp in range(4):
+            tp = ps_t.tile([P, 512], F32, name="tp", tag="xt")
+            for w in range(4):
+                s, u = 2 * sp + w // 2, w % 2
+                nc.tensor.transpose(
+                    out=tp[:, 128 * w : 128 * (w + 1)],
+                    in_=t3w[:, 256 * s + u : 256 * (s + 1) : 2],
+                    identity=idf[:],
+                )
+            dst = gt3w.rearrange("p (b x sp w) -> p sp b x w", b=16, x=8, sp=4, w=4)[:, sp]
+            src = tp[:].rearrange("p (w b x) -> p b x w", w=4, b=16, x=8)
+            if sp % 2 == 0:
+                nc.vector.tensor_copy(out=dst, in_=src)
+            else:
+                nc.scalar.copy(out=dst, in_=src)
+        quantise_unit(0)
+        nc.vector.quantize_mx(
+            out=t3_codes[:, 0:1024].bitcast(FP8X4), scales=t3_scales[:, 0:1024], in_=gt3[:]
+        )
+        permute_unit(1)
+
+        pm = const.tile([P, 2048], BF16, name="pm")
+        for b in range(4):
+            if b < 2:
+                sp = ps_y.tile([P, 512], F32, name="sp", tag="y")
+            else:
+                sp = ps_t.tile([P, 512], F32, name="sp2", tag="xt")
+            for jq in range(4):
+                j = 4 * b + jq
+                nc.tensor.matmul_mx(
+                    out=sp[:, 128 * jq : 128 * (jq + 1)],
+                    lhsT=t3_codes[:, 64 * j : 64 * j + 128].bitcast(FP8X4),
+                    lhsT_scale=t3_scales[:, 64 * j : 64 * j + 128],
+                    rhs=c4_codes[:].bitcast(FP8X4),
+                    rhs_scale=c4_scales[:],
+                    start=True,
+                    stop=True,
+                )
+            dst = pm[:].rearrange("p (tr b jq h) -> p b tr jq h", tr=16, b=4, jq=4, h=8)[:, b]
+            src = sp[:].rearrange("p (jq tr h) -> p tr jq h", jq=4, tr=16, h=8)
+            if b % 2 == 0:
+                nc.scalar.copy(out=dst, in_=src)
+            else:
+                nc.vector.tensor_copy(out=dst, in_=src)
+        transpose_unit(1)
+        permute_unit(2)
+
+        yb = ps_y.tile([P, P], F32, name="yb", tag="y")
+        nc.tensor.matmul(out=yb[:], lhsT=ones[:], rhs=bias_row[:], start=True, stop=True)
+        bias_bc = const.tile([P, P], F32, name="bias_bc")
+        nc.scalar.copy(out=bias_bc[:], in_=yb[:])
 
         gm = const.tile([P, 1024], BF16, name="gm", align_bytes=64)
         for ob in range(2):
@@ -223,40 +255,30 @@ def tile_linear2mpo_pb_t_kernel(tc, x, t3, core4, bias, out):
                 nc.tensor.transpose(
                     out=mp[:, 128 * trl : 128 * (trl + 1)], in_=pm[:, 128 * tr : 128 * (tr + 1)], identity=idb[:]
                 )
-            for e in range(2):
-                nc.vector.tensor_copy(
-                    out=gm[:].rearrange("p (g q ob ol u e) -> p ob e g q ol u", g=2, q=16, ob=2, ol=4, u=2, e=2)[:, ob, e],
-                    in_=mp[:].rearrange("p (ol e d g u q) -> p e d g q ol u", ol=4, e=2, d=2, g=2, u=2, q=16)[:, e, 0],
-                )
+            for g in range(2):
+                dst = gm[:].rearrange("p (g q ob ol u e) -> p g ob q ol u e", g=2, q=16, ob=2, ol=4, u=2, e=2)[:, g, ob]
+                src = mp[:].rearrange("p (ol e d g u q) -> p d g q ol u e", ol=4, e=2, d=2, g=2, u=2, q=16)[:, 0, g]
+                if g == 0:
+                    nc.vector.tensor_copy(out=dst, in_=src)
+                else:
+                    nc.scalar.copy(out=dst, in_=src)
+        quantise_unit(1)
         m_codes = const.tile([P, 256], U32, name="m_codes", align_bytes=64)
         m_scales = const.tile([P, 256], U8, name="m_scales", align_bytes=64)
         nc.vector.quantize_mx(out=m_codes[:].bitcast(FP8X4), scales=m_scales[:], in_=gm[:])
 
-        permute_unit(1)
-        transpose_unit(1)
-        quantise_unit(0)
-        permute_unit(2)
-
-        for i in range(2, LAST_FULL + 1):
+        for i in range(2, N_UNITS):
             transpose_unit(i)
-            if i >= 3:
-                finish_unit(i - 3)
-            quantise_unit(i - 1)
             permute_unit(i + 1)
+            if i >= 3:
+                quantise_unit(i - 1)
+                finish_unit(i - 3)
             multiply_unit(i - 2)
 
-        permute_unit(16)
-        transpose_unit(15)
-        transpose_unit(16)
-        finish_unit(12)
-        quantise_unit(14)
-        multiply_unit(13)
-        multiply_unit(14)
-        quantise_unit(15)
-        finish_unit(13)
-        quantise_unit(16)
-        multiply_unit(15)
-        multiply_unit(16)
-        finish_unit(14)
-        finish_unit(15)
-        finish_unit(16)
+        last = N_UNITS - 1
+        quantise_unit(last)
+        finish_unit(last - 2)
+        multiply_unit(last - 1)
+        multiply_unit(last)
+        finish_unit(last - 1)
+        finish_unit(last)

@@ -16,7 +16,7 @@ FLOPS = 2 * 1024 * 512 * 128 + 2 * 8192 * 1024 * 128
 UNITS = tuple((4 * c, 4) for c in range(15)) + ((60, 2), (62, 2))
 N_UNITS = len(UNITS)
 X_BUFS = 10
-SCALAR_PERMUTES = (1, 2, 4, 5, 7, 8, 10, 11, 13, 14)
+GPSIMD_PERMUTES = tuple(range(1, 15))
 STORE_AFTER = {5: 0, 8: 6, 10: 9, 12: 11, 13: 13, 14: 14, 15: 15, 16: 16}
 
 
@@ -96,8 +96,8 @@ def tile_linear2mpo_pb_t_kernel(tc, x, t3, core4, bias, out):
                 in_=x_tiles[u][:, 1024 * lo : 1024 * hi].rearrange("p (t b v j) -> p v t b j", b=16, v=4, j=16),
             )
 
-        def scalar_permute(u, t):
-            nc.scalar.copy(
+        def gpsimd_permute(u, t):
+            nc.gpsimd.tensor_copy(
                 out=permuted[u][:, 1024 * t : 1024 * (t + 1)].bitcast(F32).rearrange("p (v b j) -> p v b j", v=4, b=16, j=8),
                 in_=x_tiles[u][:, 1024 * t : 1024 * (t + 1)].bitcast(F32).rearrange("p (b v j) -> p v b j", b=16, v=4, j=8),
             )
@@ -106,9 +106,9 @@ def tile_linear2mpo_pb_t_kernel(tc, x, t3, core4, bias, out):
             if u < N_UNITS:
                 new_permuted(u)
                 nt = UNITS[u][1]
-                if u in SCALAR_PERMUTES:
+                if u in GPSIMD_PERMUTES:
                     vector_permute(u, 0, nt - 1)
-                    scalar_permute(u, nt - 1)
+                    gpsimd_permute(u, nt - 1)
                 else:
                     vector_permute(u, 0, nt)
                 load_x(u + X_BUFS)

@@ -15,8 +15,9 @@ P = 128
 FLOPS = 2 * 1024 * 512 * 128 + 2 * 8192 * 1024 * 128
 UNITS = tuple((4 * c, 4) for c in range(15)) + ((60, 2), (62, 2))
 N_UNITS = len(UNITS)
-X_BUFS = 10
-GPSIMD_PERMUTES = tuple(range(1, 15))
+X_BUFS = 9
+PERM_AT = 1
+LAG = 2
 STORE_AFTER = {5: 0, 8: 6, 10: 9, 12: 11, 13: 13, 14: 14, 15: 15, 16: 16}
 
 
@@ -88,50 +89,64 @@ def tile_linear2mpo_pb_t_kernel(tc, x, t3, core4, bias, out):
         out_sb = const.tile([P, 8192], F32, name="out_sb")
 
         def new_permuted(u):
-            permuted[u] = ppool.tile([P, 4096], BF16, name="x_perm", tag="x_perm", align_bytes=64)
+            if u < N_UNITS:
+                permuted[u] = ppool.tile([P, 4096], BF16, name="x_perm", tag="x_perm", align_bytes=64)
 
-        def vector_permute(u, lo, hi):
-            nc.vector.tensor_copy(
-                out=permuted[u][:, 1024 * lo : 1024 * hi].rearrange("p (t v b j) -> p v t b j", v=4, b=16, j=16),
-                in_=x_tiles[u][:, 1024 * lo : 1024 * hi].rearrange("p (t b v j) -> p v t b j", b=16, v=4, j=16),
+        def permute(copy, u, lo, hi):
+            copy(
+                out=permuted[u][:, 512 * lo : 512 * hi].rearrange("p (tg h b j) -> p h tg b j", h=2, b=16, j=16),
+                in_=x_tiles[u][:, 512 * lo : 512 * hi].rearrange("p (tg b h j) -> p h tg b j", b=16, h=2, j=16),
             )
 
-        def gpsimd_permute(u, t):
-            nc.gpsimd.tensor_copy(
-                out=permuted[u][:, 1024 * t : 1024 * (t + 1)].bitcast(F32).rearrange("p (v b j) -> p v b j", v=4, b=16, j=8),
-                in_=x_tiles[u][:, 1024 * t : 1024 * (t + 1)].bitcast(F32).rearrange("p (b v j) -> p v b j", b=16, v=4, j=8),
-            )
+        def scalar_permute(u):
+            if 3 <= u < N_UNITS:
+                n = 2 * UNITS[u][1]
+                nc.scalar.copy(
+                    out=permuted[u][:, 512 * (n - 1) : 512 * n].bitcast(F32).rearrange("p (h b j) -> p h b j", h=2, b=16, j=8),
+                    in_=x_tiles[u][:, 512 * (n - 1) : 512 * n].bitcast(F32).rearrange("p (b h j) -> p h b j", b=16, h=2, j=8),
+                )
 
         def permute_unit(u):
             if u < N_UNITS:
-                new_permuted(u)
-                nt = UNITS[u][1]
-                if u in GPSIMD_PERMUTES:
-                    vector_permute(u, 0, nt - 1)
-                    gpsimd_permute(u, nt - 1)
-                else:
-                    vector_permute(u, 0, nt)
+                lo = 2 if gpsimd_helps(u) else 0
+                if lo:
+                    nc.gpsimd.tensor_copy(
+                        out=permuted[u][:, 0:1024].bitcast(F32).rearrange("p (g h b j) -> p h g b j", g=2, h=2, b=16, j=8),
+                        in_=x_tiles[u][:, 0:1024].bitcast(F32).rearrange("p (g b h j) -> p h g b j", g=2, b=16, h=2, j=8),
+                    )
+                permute(nc.vector.tensor_copy, u, lo, 2 * UNITS[u][1] - (1 if u >= 3 else 0))
                 load_x(u + X_BUFS)
 
-        def transpose_tile(u, t, copy):
-            xw = permuted[u][:].bitcast(F32)
+        def transpose_tile(u, t):
             bank = ps_t.tile([P, 512], F32, name="xt", tag="xt")
             for a in range(4):
                 w0 = 512 * t + 128 * a
-                nc.tensor.transpose(out=bank[:, 128 * a : 128 * (a + 1)], in_=xw[:, w0 : w0 + 128], identity=idf[:])
+                nc.tensor.transpose(
+                    out=bank[:, 128 * a : 128 * (a + 1)],
+                    in_=permuted[u][:].bitcast(F32)[:, w0 : w0 + 128],
+                    identity=idf[:],
+                )
+            return bank
+
+        def copy_tile(u, t, bank):
             gw = grouped[u][:].bitcast(F32)
-            copy(
-                out=gw[:, 512 * t : 512 * (t + 1)].rearrange("p (g r u) -> p g r u", g=2, r=128, u=2),
-                in_=bank[:].rearrange("p (g u r) -> p g r u", g=2, u=2, r=128),
+            nc.scalar.copy(
+                out=gw[:, 512 * t : 512 * (t + 1)].rearrange("p (g r h) -> p g r h", g=2, r=128, h=2),
+                in_=bank[:].rearrange("p (g h r) -> p g r h", g=2, h=2, r=128),
             )
 
-        def new_grouped(u):
-            grouped[u] = gpool.tile([P, 4096], BF16, name="g_sb", tag="g_sb", align_bytes=64)
+        def gpsimd_helps(u):
+            return u > 1 and UNITS[u][1] == 4
 
         def transpose_unit(u):
-            new_grouped(u)
-            for t in range(UNITS[u][1]):
-                transpose_tile(u, t, nc.scalar.copy)
+            nt = UNITS[u][1]
+            new_permuted(u + 1)
+            grouped[u] = gpool.tile([P, 4096], BF16, name="g_sb", tag="g_sb", align_bytes=64)
+            order = (1, 2, 3, 0) if gpsimd_helps(u) else range(nt)
+            for k, t in enumerate(order):
+                copy_tile(u, t, transpose_tile(u, t))
+                if k == PERM_AT:
+                    scalar_permute(u + 1)
 
         def quantise_unit(u):
             nt = UNITS[u][1]
@@ -175,110 +190,137 @@ def tile_linear2mpo_pb_t_kernel(tc, x, t3, core4, bias, out):
                 hi = 128 * (t0 + nt)
                 nc.sync.dma_start(out=out_v[:, lo:hi], in_=out_sb[:, lo:hi])
 
-        new_permuted(0)
-        new_grouped(0)
-        for t in range(4):
-            vector_permute(0, t, t + 1)
-            transpose_tile(0, t, nc.scalar.copy)
-        load_x(X_BUFS)
-
-        gc4 = const.tile([P, 512], BF16, name="gc4", align_bytes=64)
-        for e in range(2):
-            nc.vector.tensor_copy(
-                out=gc4[:].rearrange("p (o e h t) -> p e o h t", o=8, e=2, h=8, t=4)[:, e],
-                in_=c4raw[:].rearrange("p (t h e o) -> p e o h t", t=4, h=8, e=2, o=8)[:, e],
-            )
         c4_codes = const.tile([P, 128], U32, name="c4_codes", align_bytes=64)
         c4_scales = const.tile([P, 128], U8, name="c4_scales", align_bytes=64)
-        nc.vector.quantize_mx(out=c4_codes[:].bitcast(FP8X4), scales=c4_scales[:], in_=gc4[:])
-
-        t3w = t3_sb[:].bitcast(F32)
         gt3 = const.tile([P, 4096], BF16, name="gt3", align_bytes=64)
-        gt3w = gt3[:].bitcast(F32)
-        for sp in range(4):
-            tp = ps_t.tile([P, 512], F32, name="tp", tag="xt")
-            for w in range(4):
-                s, u = 2 * sp + w // 2, w % 2
-                nc.tensor.transpose(
-                    out=tp[:, 128 * w : 128 * (w + 1)],
-                    in_=t3w[:, 256 * s + u : 256 * (s + 1) : 2],
-                    identity=idf[:],
-                )
-            dst = gt3w.rearrange("p (b x sp w) -> p sp b x w", b=16, x=8, sp=4, w=4)[:, sp]
-            src = tp[:].rearrange("p (w b x) -> p b x w", w=4, b=16, x=8)
-            if sp % 2 == 0:
-                nc.vector.tensor_copy(out=dst, in_=src)
-            else:
-                nc.scalar.copy(out=dst, in_=src)
-        quantise_unit(0)
-        nc.vector.quantize_mx(
-            out=t3_codes[:, 0:1024].bitcast(FP8X4), scales=t3_scales[:, 0:1024], in_=gt3[:]
-        )
-        permute_unit(1)
-
-        pm = const.tile([P, 2048], BF16, name="pm")
-        for b in range(4):
-            if b < 2:
-                sp = ps_y.tile([P, 512], F32, name="sp", tag="y")
-            else:
-                sp = ps_t.tile([P, 512], F32, name="sp2", tag="xt")
-            for jq in range(4):
-                j = 4 * b + jq
-                nc.tensor.matmul_mx(
-                    out=sp[:, 128 * jq : 128 * (jq + 1)],
-                    lhsT=t3_codes[:, 64 * j : 64 * j + 128].bitcast(FP8X4),
-                    lhsT_scale=t3_scales[:, 64 * j : 64 * j + 128],
-                    rhs=c4_codes[:].bitcast(FP8X4),
-                    rhs_scale=c4_scales[:],
-                    start=True,
-                    stop=True,
-                )
-            dst = pm[:].rearrange("p (tr b jq h) -> p b tr jq h", tr=16, b=4, jq=4, h=8)[:, b]
-            src = sp[:].rearrange("p (jq tr h) -> p tr jq h", jq=4, tr=16, h=8)
-            if b % 2 == 0:
-                nc.scalar.copy(out=dst, in_=src)
-            else:
-                nc.vector.tensor_copy(out=dst, in_=src)
-        transpose_unit(1)
-        permute_unit(2)
-
-        yb = ps_y.tile([P, P], F32, name="yb", tag="y")
-        nc.tensor.matmul(out=yb[:], lhsT=ones[:], rhs=bias_row[:], start=True, stop=True)
         bias_bc = const.tile([P, P], F32, name="bias_bc")
-        nc.scalar.copy(out=bias_bc[:], in_=yb[:])
-
+        pm = const.tile([P, 2048], BF16, name="pm")
         gm = const.tile([P, 1024], BF16, name="gm", align_bytes=64)
-        for ob in range(2):
-            mp = ps_t.tile([P, 1024], BF16, name="mp", tag="xt")
-            for trl in range(8):
-                tr = 8 * ob + trl
-                nc.tensor.transpose(
-                    out=mp[:, 128 * trl : 128 * (trl + 1)], in_=pm[:, 128 * tr : 128 * (tr + 1)], identity=idb[:]
+        m_codes = const.tile([P, 256], U32, name="m_codes", align_bytes=64)
+        m_scales = const.tile([P, 256], U8, name="m_scales", align_bytes=64)
+
+        def quantise_core4():
+            gc4 = const.tile([P, 512], BF16, name="gc4", align_bytes=64)
+            for e in range(2):
+                nc.vector.tensor_copy(
+                    out=gc4[:].rearrange("p (o e h t) -> p e o h t", o=8, e=2, h=8, t=4)[:, e],
+                    in_=c4raw[:].rearrange("p (t h e o) -> p e o h t", t=4, h=8, e=2, o=8)[:, e],
                 )
-            for g in range(2):
-                dst = gm[:].rearrange("p (g q ob ol u e) -> p g ob q ol u e", g=2, q=16, ob=2, ol=4, u=2, e=2)[:, g, ob]
-                src = mp[:].rearrange("p (ol e d g u q) -> p d g q ol u e", ol=4, e=2, d=2, g=2, u=2, q=16)[:, 0, g]
-                if g == 0:
+            nc.vector.quantize_mx(out=c4_codes[:].bitcast(FP8X4), scales=c4_scales[:], in_=gc4[:])
+
+        def transpose_t3():
+            t3w = t3_sb[:].bitcast(F32)
+            gt3w = gt3[:].bitcast(F32)
+            for sp in range(4):
+                tp = ps_t.tile([P, 512], F32, name="tp", tag="xt")
+                for w in range(4):
+                    s, u = 2 * sp + w // 2, w % 2
+                    nc.tensor.transpose(
+                        out=tp[:, 128 * w : 128 * (w + 1)],
+                        in_=t3w[:, 256 * s + u : 256 * (s + 1) : 2],
+                        identity=idf[:],
+                    )
+                dst = gt3w.rearrange("p (bu g h sp w) -> p sp bu g h w", bu=32, g=2, h=2, sp=4, w=4)[:, sp]
+                src = tp[:].rearrange("p (w g bu h) -> p bu g h w", w=4, g=2, bu=32, h=2)
+                nc.scalar.copy(out=dst, in_=src)
+
+        def quantise_t3():
+            nc.vector.quantize_mx(
+                out=t3_codes[:, 0:1024].bitcast(FP8X4), scales=t3_scales[:, 0:1024], in_=gt3[:]
+            )
+
+        def spread_bias():
+            yb = ps_y.tile([P, P], F32, name="yb", tag="y")
+            nc.tensor.matmul(out=yb[:], lhsT=ones[:], rhs=bias_row[:], start=True, stop=True)
+            nc.scalar.copy(out=bias_bc[:], in_=yb[:])
+
+        def first_contraction():
+            for b in range(4):
+                if b < 2:
+                    sp = ps_y.tile([P, 512], F32, name="sp", tag="y")
+                else:
+                    sp = ps_t.tile([P, 512], F32, name="sp2", tag="xt")
+                for jq in range(4):
+                    j = 4 * b + jq
+                    nc.tensor.matmul_mx(
+                        out=sp[:, 128 * jq : 128 * (jq + 1)],
+                        lhsT=t3_codes[:, 64 * j : 64 * j + 128].bitcast(FP8X4),
+                        lhsT_scale=t3_scales[:, 64 * j : 64 * j + 128],
+                        rhs=c4_codes[:].bitcast(FP8X4),
+                        rhs_scale=c4_scales[:],
+                        start=True,
+                        stop=True,
+                    )
+                dst = pm[:].rearrange("p (tr b jq h) -> p b tr jq h", tr=16, b=4, jq=4, h=8)[:, b]
+                src = sp[:].rearrange("p (jq tr h) -> p tr jq h", jq=4, tr=16, h=8)
+                if b % 2 == 0:
+                    nc.scalar.copy(out=dst, in_=src)
+                else:
+                    nc.vector.tensor_copy(out=dst, in_=src)
+
+        def transpose_m():
+            for ob in range(2):
+                mp = ps_t.tile([P, 1024], BF16, name="mp", tag="xt")
+                for trl in range(8):
+                    tr = 8 * ob + trl
+                    nc.tensor.transpose(
+                        out=mp[:, 128 * trl : 128 * (trl + 1)], in_=pm[:, 128 * tr : 128 * (tr + 1)], identity=idb[:]
+                    )
+                dst = gm[:].rearrange("p (q ob ol h e) -> p ob q ol h e", q=32, ob=2, ol=4, h=2, e=2)[:, ob]
+                src = mp[:].rearrange("p (ol e d h q) -> p d q ol h e", ol=4, e=2, d=2, h=2, q=32)[:, 0]
+                if ob == 0:
                     nc.vector.tensor_copy(out=dst, in_=src)
                 else:
                     nc.scalar.copy(out=dst, in_=src)
-        quantise_unit(1)
-        m_codes = const.tile([P, 256], U32, name="m_codes", align_bytes=64)
-        m_scales = const.tile([P, 256], U8, name="m_scales", align_bytes=64)
-        nc.vector.quantize_mx(out=m_codes[:].bitcast(FP8X4), scales=m_scales[:], in_=gm[:])
 
-        for i in range(2, N_UNITS):
-            transpose_unit(i)
-            permute_unit(i + 1)
-            if i >= 3:
-                quantise_unit(i - 1)
-                finish_unit(i - 3)
-            multiply_unit(i - 2)
+        def quantise_m():
+            nc.vector.quantize_mx(out=m_codes[:].bitcast(FP8X4), scales=m_scales[:], in_=gm[:])
+
+        multiplied = []
+        finished = []
+
+        def multiply_up_to(last, count):
+            for u in range(len(multiplied), min(len(multiplied) + count, last + 1)):
+                multiply_unit(u)
+                multiplied.append(u)
+
+        def finish_multiplied():
+            for u in range(len(finished), len(multiplied)):
+                finish_unit(u)
+                finished.append(u)
+
+        new_permuted(0)
+        for t in range(4):
+            permute(nc.vector.tensor_copy, 0, 2 * t, 2 * t + 2)
+        load_x(X_BUFS)
+
+        for i in range(N_UNITS):
+            if i == 0:
+                transpose_unit(0)
+                quantise_core4()
+                transpose_t3()
+                quantise_unit(0)
+                quantise_t3()
+                permute_unit(1)
+                first_contraction()
+            elif i == 1:
+                transpose_unit(1)
+                permute_unit(2)
+                spread_bias()
+                transpose_m()
+                quantise_unit(1)
+                quantise_m()
+            else:
+                transpose_unit(i)
+                finish_multiplied()
+                permute_unit(i + 1)
+                if i > 2:
+                    quantise_unit(i - 1)
+                multiply_up_to(i - LAG, 1)
 
         last = N_UNITS - 1
+        finish_multiplied()
         quantise_unit(last)
-        finish_unit(last - 2)
-        multiply_unit(last - 1)
-        multiply_unit(last)
-        finish_unit(last - 1)
-        finish_unit(last)
+        while len(finished) < N_UNITS:
+            finish_multiplied()
+            multiply_up_to(last, 2)

@@ -70,15 +70,15 @@ def tile_linear2mpo_pb_t_kernel(tc, x, t3, core4, bias, out):
                 new_x(u)
                 load_x_tiles(u, 0, UNITS[u][1])
 
+        t3_sb = const.tile([P, 4096], BF16, name="t3_sb")
+        for sp in range(4):
+            nc.sync.dma_start(out=t3_sb[:, 1024 * sp : 1024 * (sp + 1)], in_=t3_v[:, 1024 * sp : 1024 * (sp + 1)])
+        c4raw = const.tile([P, 512], BF16, name="c4raw")
+        nc.sync.dma_start(out=c4raw[:], in_=c4_v)
         new_x(0)
         for t in range(4):
             load_x_tiles(0, t, t + 1)
         nc.sync.dma_start(out=bias_row[0:1, :], in_=bias_v)
-        c4raw = const.tile([P, 512], BF16, name="c4raw")
-        nc.sync.dma_start(out=c4raw[:], in_=c4_v)
-        t3_sb = const.tile([P, 4096], BF16, name="t3_sb")
-        for sp in range(4):
-            nc.sync.dma_start(out=t3_sb[:, 1024 * sp : 1024 * (sp + 1)], in_=t3_v[:, 1024 * sp : 1024 * (sp + 1)])
         for u in range(1, X_BUFS):
             load_x(u)
 
@@ -94,12 +94,12 @@ def tile_linear2mpo_pb_t_kernel(tc, x, t3, core4, bias, out):
 
         def permute(copy, u, lo, hi):
             copy(
-                out=permuted[u][:, 512 * lo : 512 * hi].rearrange("p (tg h b j) -> p h tg b j", h=2, b=16, j=16),
-                in_=x_tiles[u][:, 512 * lo : 512 * hi].rearrange("p (tg b h j) -> p h tg b j", b=16, h=2, j=16),
+                out=permuted[u][:, 512 * lo : 512 * hi].rearrange("p (tg h b j) -> p b tg h j", h=2, b=16, j=16),
+                in_=x_tiles[u][:, 512 * lo : 512 * hi].rearrange("p (tg b h j) -> p b tg h j", b=16, h=2, j=16),
             )
 
         def scalar_permute(u):
-            if 3 <= u < N_UNITS:
+            if 2 <= u < N_UNITS:
                 n = 2 * UNITS[u][1]
                 nc.scalar.copy(
                     out=permuted[u][:, 512 * (n - 1) : 512 * n].bitcast(F32).rearrange("p (h b j) -> p h b j", h=2, b=16, j=8),
@@ -114,7 +114,7 @@ def tile_linear2mpo_pb_t_kernel(tc, x, t3, core4, bias, out):
                         out=permuted[u][:, 0:1024].bitcast(F32).rearrange("p (g h b j) -> p h g b j", g=2, h=2, b=16, j=8),
                         in_=x_tiles[u][:, 0:1024].bitcast(F32).rearrange("p (g b h j) -> p h g b j", g=2, b=16, h=2, j=8),
                     )
-                permute(nc.vector.tensor_copy, u, lo, 2 * UNITS[u][1] - (1 if u >= 3 else 0))
+                permute(nc.vector.tensor_copy, u, lo, 2 * UNITS[u][1] - (1 if u >= 2 else 0))
                 load_x(u + X_BUFS)
 
         def transpose_tile(u, t):
@@ -162,7 +162,10 @@ def tile_linear2mpo_pb_t_kernel(tc, x, t3, core4, bias, out):
         def multiply_unit(u):
             nt = UNITS[u][1]
             x_codes, x_scales = codes[u]
-            y = ps_y.tile([P, 512], F32, name="y", tag="y")
+            if u == N_UNITS - 1:
+                y = ps_t.tile([P, 512], F32, name="y_last", tag="xt")
+            else:
+                y = ps_y.tile([P, 512], F32, name="y", tag="y")
             for t in range(nt):
                 for g in range(2):
                     s0 = 128 * (2 * t + g)
@@ -222,7 +225,10 @@ def tile_linear2mpo_pb_t_kernel(tc, x, t3, core4, bias, out):
                     )
                 dst = gt3w.rearrange("p (bu g h sp w) -> p sp bu g h w", bu=32, g=2, h=2, sp=4, w=4)[:, sp]
                 src = tp[:].rearrange("p (w g bu h) -> p bu g h w", w=4, g=2, bu=32, h=2)
-                nc.scalar.copy(out=dst, in_=src)
+                if sp % 2 == 0:
+                    nc.vector.tensor_copy(out=dst, in_=src)
+                else:
+                    nc.scalar.copy(out=dst, in_=src)
 
         def quantise_t3():
             nc.vector.quantize_mx(
@@ -289,37 +295,31 @@ def tile_linear2mpo_pb_t_kernel(tc, x, t3, core4, bias, out):
                 finish_unit(u)
                 finished.append(u)
 
+        transpose_t3()
+        quantise_core4()
         new_permuted(0)
+        quantise_t3()
         for t in range(4):
             permute(nc.vector.tensor_copy, 0, 2 * t, 2 * t + 2)
         load_x(X_BUFS)
-
         for i in range(N_UNITS):
             if i == 0:
-                transpose_unit(0)
-                quantise_core4()
-                transpose_t3()
-                quantise_unit(0)
-                quantise_t3()
-                permute_unit(1)
                 first_contraction()
-            elif i == 1:
-                transpose_unit(1)
-                permute_unit(2)
+                transpose_unit(0)
+                permute_unit(1)
                 spread_bias()
                 transpose_m()
-                quantise_unit(1)
+                quantise_unit(0)
                 quantise_m()
             else:
                 transpose_unit(i)
                 finish_multiplied()
                 permute_unit(i + 1)
-                if i > 2:
+                if i > 1:
                     quantise_unit(i - 1)
                 multiply_up_to(i - LAG, 1)
 
         last = N_UNITS - 1
-        finish_multiplied()
         quantise_unit(last)
         while len(finished) < N_UNITS:
             finish_multiplied()

from contextlib import ExitStack

import concourse.mybir as mybir
from concourse.masks import make_identity

F32 = mybir.dt.float32
BF16 = mybir.dt.bfloat16
U32 = mybir.dt.uint32
U8 = mybir.dt.uint8
I32 = mybir.dt.int32
FP8X4 = mybir.dt.float8_e4m3fn_x4
ADD = mybir.AluOpType.add

P = 128
FLOPS = 2 * 1024 * 512 * 128 + 2 * 8192 * 1024 * 128
UNITS = tuple((4 * c, 4) for c in range(15)) + ((60, 2), (62, 2))
N_UNITS = len(UNITS)
X_BUFS = 9
PERM_AT = 1
LAG = 2
STORE_AFTER = {5: 0, 8: 6, 10: 9, 12: 11, 13: 13, 14: 14, 15: 15, 16: 16}


def tile_linear2mpo_pb_t_kernel(tc, x, t3, core4, bias, out):
    nc = tc.nc
    with ExitStack() as ctx:
        const = ctx.enter_context(tc.tile_pool(name="const", bufs=1))
        xpool = ctx.enter_context(tc.tile_pool(name="xpool", bufs=X_BUFS))
        ppool = ctx.enter_context(tc.tile_pool(name="ppool", bufs=2))
        gpool = ctx.enter_context(tc.tile_pool(name="gpool", bufs=3))
        cpool = ctx.enter_context(tc.tile_pool(name="cpool", bufs=6))
        ps_t = ctx.enter_context(tc.psum_pool(name="ps_t", bufs=6))
        ps_y = ctx.enter_context(tc.psum_pool(name="ps_y", bufs=2))
        ctx.enter_context(tc.manual_schedule())

        x_v = x.rearrange("b (q t) k -> (b q) (t k)", t=64)
        out_v = out.rearrange("b (q t) n -> (b q) (t n)", t=64)
        t3_v = t3.rearrange("a (h s) r -> (a h) (s r)", h=2)
        c4_v = core4.rearrange("(q t) i o z -> q (t i o z)", t=4)
        bias_v = bias.rearrange("(o n) -> o n", o=1)

        idf = const.tile([P, P], F32, name="idf")
        make_identity(nc, idf[:])
        idb = const.tile([P, P], BF16, name="idb")
        make_identity(nc, idb[:])
        bias_row = const.tile([P, P], BF16, name="bias_row")
        nc.vector.memset(bias_row[:], 0.0)
        ones = const.tile([P, P], BF16, name="ones")
        nc.vector.memset(ones[:], 1.0)
        warm = const.tile([P, 16], BF16, name="warm")
        nc.scalar.copy(out=warm[:], in_=ones[:, 0:16])
        t3_codes = const.tile([P, 1088], U32, name="t3_codes", align_bytes=64)
        t3_scales = const.tile([P, 1088], U8, name="t3_scales", align_bytes=64)
        nc.vector.memset(t3_codes[:, 1024:1088].bitcast(I32), 0)
        nc.vector.memset(t3_scales[:, 1024:1088].bitcast(I32), 0)

        x_tiles = {}

        def new_x(u):
            x_tiles[u] = xpool.tile([P, 4096], BF16, name="x_sb", tag="x_sb")

        def load_x_tiles(u, lo, hi):
            t0 = UNITS[u][0]
            nc.sync.dma_start(
                out=x_tiles[u][:, 1024 * lo : 1024 * hi], in_=x_v[:, 1024 * (t0 + lo) : 1024 * (t0 + hi)]
            )

        def load_x(u):
            if u < N_UNITS:
                new_x(u)
                load_x_tiles(u, 0, UNITS[u][1])

        t3_sb = const.tile([P, 4096], BF16, name="t3_sb")
        for sp in range(4):
            nc.sync.dma_start(out=t3_sb[:, 1024 * sp : 1024 * (sp + 1)], in_=t3_v[:, 1024 * sp : 1024 * (sp + 1)])
        c4raw = const.tile([P, 512], BF16, name="c4raw")
        nc.sync.dma_start(out=c4raw[:], in_=c4_v)
        new_x(0)
        for t in range(4):
            load_x_tiles(0, t, t + 1)
        nc.sync.dma_start(out=bias_row[0:1, :], in_=bias_v)
        for u in range(1, X_BUFS):
            load_x(u)

        permuted = {}
        grouped = {}
        codes = {}
        y_tiles = {}
        out_sb = const.tile([P, 8192], F32, name="out_sb")

        def new_permuted(u):
            if u < N_UNITS:
                permuted[u] = ppool.tile([P, 4096], BF16, name="x_perm", tag="x_perm", align_bytes=64)

        def permute(copy, u, lo, hi):
            copy(
                out=permuted[u][:, 512 * lo : 512 * hi].rearrange("p (tg h b j) -> p b tg h j", h=2, b=16, j=16),
                in_=x_tiles[u][:, 512 * lo : 512 * hi].rearrange("p (tg b h j) -> p b tg h j", b=16, h=2, j=16),
            )

        def scalar_permute(u):
            if 2 <= u < N_UNITS:
                n = 2 * UNITS[u][1]
                nc.scalar.copy(
                    out=permuted[u][:, 512 * (n - 1) : 512 * n].bitcast(F32).rearrange("p (h b j) -> p h b j", h=2, b=16, j=8),
                    in_=x_tiles[u][:, 512 * (n - 1) : 512 * n].bitcast(F32).rearrange("p (b h j) -> p h b j", b=16, h=2, j=8),
                )

        def permute_unit(u):
            if u < N_UNITS:
                lo = 2 if gpsimd_helps(u) else 0
                if lo:
                    nc.gpsimd.tensor_copy(
                        out=permuted[u][:, 0:1024].bitcast(F32).rearrange("p (g h b j) -> p h g b j", g=2, h=2, b=16, j=8),
                        in_=x_tiles[u][:, 0:1024].bitcast(F32).rearrange("p (g b h j) -> p h g b j", g=2, b=16, h=2, j=8),
                    )
                permute(nc.vector.tensor_copy, u, lo, 2 * UNITS[u][1] - (1 if u >= 2 else 0))
                load_x(u + X_BUFS)

        def transpose_tile(u, t):
            bank = ps_t.tile([P, 512], F32, name="xt", tag="xt")
            for a in range(4):
                w0 = 512 * t + 128 * a
                nc.tensor.transpose(
                    out=bank[:, 128 * a : 128 * (a + 1)],
                    in_=permuted[u][:].bitcast(F32)[:, w0 : w0 + 128],
                    identity=idf[:],
                )
            return bank

        def copy_tile(u, t, bank):
            gw = grouped[u][:].bitcast(F32)
            nc.scalar.copy(
                out=gw[:, 512 * t : 512 * (t + 1)].rearrange("p (g r h) -> p g r h", g=2, r=128, h=2),
                in_=bank[:].rearrange("p (g h r) -> p g r h", g=2, h=2, r=128),
            )

        def gpsimd_helps(u):
            return u > 1 and UNITS[u][1] == 4

        def transpose_unit(u):
            nt = UNITS[u][1]
            new_permuted(u + 1)
            grouped[u] = gpool.tile([P, 4096], BF16, name="g_sb", tag="g_sb", align_bytes=64)
            order = (1, 2, 3, 0) if gpsimd_helps(u) else range(nt)
            for k, t in enumerate(order):
                copy_tile(u, t, transpose_tile(u, t))
                if k == PERM_AT:
                    scalar_permute(u + 1)

        def quantise_unit(u):
            nt = UNITS[u][1]
            x_codes = cpool.tile([P, 1024], U32, name="x_codes", tag="x_codes", align_bytes=64)
            x_scales = cpool.tile([P, 1024], U8, name="x_scales", tag="x_scales", align_bytes=64)
            nc.vector.quantize_mx(
                out=x_codes[:, 0 : 256 * nt].bitcast(FP8X4),
                scales=x_scales[:, 0 : 256 * nt],
                in_=grouped[u][:, 0 : 1024 * nt],
            )
            codes[u] = (x_codes, x_scales)

        def multiply_unit(u):
            nt = UNITS[u][1]
            x_codes, x_scales = codes[u]
            if u == N_UNITS - 1:
                y = ps_t.tile([P, 512], F32, name="y_last", tag="xt")
            else:
                y = ps_y.tile([P, 512], F32, name="y", tag="y")
            for t in range(nt):
                for g in range(2):
                    s0 = 128 * (2 * t + g)
                    nc.tensor.matmul_mx(
                        out=y[:, 128 * t : 128 * (t + 1)],
                        lhsT=x_codes[:, s0 : s0 + 128].bitcast(FP8X4),
                        lhsT_scale=x_scales[:, s0 : s0 + 128],
                        rhs=m_codes[:, 128 * g : 128 * (g + 1)].bitcast(FP8X4),
                        rhs_scale=m_scales[:, 128 * g : 128 * (g + 1)],
                        start=(g == 0),
                        stop=(g == 1),
                    )
            y_tiles[u] = y

        def finish_unit(u):
            t0, nt = UNITS[u]
            nc.vector.tensor_tensor(
                out=out_sb[:, 128 * t0 : 128 * (t0 + nt)].rearrange("p (t n) -> p t n", n=128),
                in0=y_tiles[u][:, 0 : 128 * nt].rearrange("p (t n) -> p t n", n=128),
                in1=bias_bc[:].unsqueeze(1).to_broadcast([P, nt, 128]),
                op=ADD,
            )
            if u in STORE_AFTER:
                lo = 128 * UNITS[STORE_AFTER[u]][0]
                hi = 128 * (t0 + nt)
                nc.sync.dma_start(out=out_v[:, lo:hi], in_=out_sb[:, lo:hi])

        c4_codes = const.tile([P, 128], U32, name="c4_codes", align_bytes=64)
        c4_scales = const.tile([P, 128], U8, name="c4_scales", align_bytes=64)
        gt3 = const.tile([P, 4096], BF16, name="gt3", align_bytes=64)
        bias_bc = const.tile([P, P], F32, name="bias_bc")
        pm = const.tile([P, 2048], BF16, name="pm")
        gm = const.tile([P, 1024], BF16, name="gm", align_bytes=64)
        m_codes = const.tile([P, 256], U32, name="m_codes", align_bytes=64)
        m_scales = const.tile([P, 256], U8, name="m_scales", align_bytes=64)

        def quantise_core4():
            gc4 = const.tile([P, 512], BF16, name="gc4", align_bytes=64)
            for e in range(2):
                nc.vector.tensor_copy(
                    out=gc4[:].rearrange("p (o e h t) -> p e o h t", o=8, e=2, h=8, t=4)[:, e],
                    in_=c4raw[:].rearrange("p (t h e o) -> p e o h t", t=4, h=8, e=2, o=8)[:, e],
                )
            nc.vector.quantize_mx(out=c4_codes[:].bitcast(FP8X4), scales=c4_scales[:], in_=gc4[:])

        def transpose_t3():
            t3w = t3_sb[:].bitcast(F32)
            gt3w = gt3[:].bitcast(F32)
            for sp in range(4):
                tp = ps_t.tile([P, 512], F32, name="tp", tag="xt")
                for w in range(4):
                    s, u = 2 * sp + w // 2, w % 2
                    nc.tensor.transpose(
                        out=tp[:, 128 * w : 128 * (w + 1)],
                        in_=t3w[:, 256 * s + u : 256 * (s + 1) : 2],
                        identity=idf[:],
                    )
                dst = gt3w.rearrange("p (bu g h sp w) -> p sp bu g h w", bu=32, g=2, h=2, sp=4, w=4)[:, sp]
                src = tp[:].rearrange("p (w g bu h) -> p bu g h w", w=4, g=2, bu=32, h=2)
                if sp % 2 == 0:
                    nc.vector.tensor_copy(out=dst, in_=src)
                else:
                    nc.scalar.copy(out=dst, in_=src)

        def quantise_t3():
            nc.vector.quantize_mx(
                out=t3_codes[:, 0:1024].bitcast(FP8X4), scales=t3_scales[:, 0:1024], in_=gt3[:]
            )

        def spread_bias():
            yb = ps_y.tile([P, P], F32, name="yb", tag="y")
            nc.tensor.matmul(out=yb[:], lhsT=ones[:], rhs=bias_row[:], start=True, stop=True)
            nc.scalar.copy(out=bias_bc[:], in_=yb[:])

        def first_contraction():
            for b in range(4):
                if b < 2:
                    sp = ps_y.tile([P, 512], F32, name="sp", tag="y")
                else:
                    sp = ps_t.tile([P, 512], F32, name="sp2", tag="xt")
                for jq in range(4):
                    j = 4 * b + jq
                    nc.tensor.matmul_mx(
                        out=sp[:, 128 * jq : 128 * (jq + 1)],
                        lhsT=t3_codes[:, 64 * j : 64 * j + 128].bitcast(FP8X4),
                        lhsT_scale=t3_scales[:, 64 * j : 64 * j + 128],
                        rhs=c4_codes[:].bitcast(FP8X4),
                        rhs_scale=c4_scales[:],
                        start=True,
                        stop=True,
                    )
                dst = pm[:].rearrange("p (tr b jq h) -> p b tr jq h", tr=16, b=4, jq=4, h=8)[:, b]
                src = sp[:].rearrange("p (jq tr h) -> p tr jq h", jq=4, tr=16, h=8)
                if b % 2 == 0:
                    nc.scalar.copy(out=dst, in_=src)
                else:
                    nc.vector.tensor_copy(out=dst, in_=src)

        def transpose_m():
            for ob in range(2):
                mp = ps_t.tile([P, 1024], BF16, name="mp", tag="xt")
                for trl in range(8):
                    tr = 8 * ob + trl
                    nc.tensor.transpose(
                        out=mp[:, 128 * trl : 128 * (trl + 1)], in_=pm[:, 128 * tr : 128 * (tr + 1)], identity=idb[:]
                    )
                dst = gm[:].rearrange("p (q ob ol h e) -> p ob q ol h e", q=32, ob=2, ol=4, h=2, e=2)[:, ob]
                src = mp[:].rearrange("p (ol e d h q) -> p d q ol h e", ol=4, e=2, d=2, h=2, q=32)[:, 0]
                if ob == 0:
                    nc.vector.tensor_copy(out=dst, in_=src)
                else:
                    nc.scalar.copy(out=dst, in_=src)

        def quantise_m():
            nc.vector.quantize_mx(out=m_codes[:].bitcast(FP8X4), scales=m_scales[:], in_=gm[:])

        multiplied = []
        finished = []

        def multiply_up_to(last, count):
            for u in range(len(multiplied), min(len(multiplied) + count, last + 1)):
                multiply_unit(u)
                multiplied.append(u)

        def finish_multiplied():
            for u in range(len(finished), len(multiplied)):
                finish_unit(u)
                finished.append(u)

        transpose_t3()
        quantise_core4()
        new_permuted(0)
        quantise_t3()
        for t in range(4):
            permute(nc.vector.tensor_copy, 0, 2 * t, 2 * t + 2)
        load_x(X_BUFS)
        for i in range(N_UNITS):
            if i == 0:
                first_contraction()
                transpose_unit(0)
                permute_unit(1)
                spread_bias()
                transpose_m()
                quantise_unit(0)
                quantise_m()
            else:
                transpose_unit(i)
                finish_multiplied()
                permute_unit(i + 1)
                if i > 1:
                    quantise_unit(i - 1)
                multiply_up_to(i - LAG, 1)

        last = N_UNITS - 1
        quantise_unit(last)
        while len(finished) < N_UNITS:
            finish_multiplied()
            multiply_up_to(last, 2)
